import numpy as np
import ml_dtypes

BF16 = ml_dtypes.bfloat16


def bf(x):
    return np.asarray(x, np.float32).astype(BF16)


def f32(x):
    return np.asarray(x, np.float32)


def f64(x):
    return np.asarray(x).astype(np.float64)


def striped(idx):
    return np.tile(idx.reshape(-1, 16).T, (8, 1))


C, D, HALF, S, N = 256, 128, 64, 512, 256


def rotate_half(x):
    return np.concatenate([-x[:, HALF:], x[:, :HALF]], axis=1)


def setup_inputs():
    base = f32(np.random.standard_normal((C, S)))
    k = f32(np.random.standard_normal((C, N)))
    ang = np.random.uniform(-1.5, 1.5, (HALF, N))
    theta = f32(np.concatenate([ang, ang], axis=0))
    return {"base": base, "k": k, "theta": theta, "offs": striped(np.random.permutation(S)[:N])}


def reference(base, k, theta, offs):
    idx = offs[:16].T.reshape(-1)
    kh = f64(k).reshape(C // D, D, N)
    th = f64(theta)[None, :, :]
    new = kh * np.cos(th) + rotate_half(kh) * np.sin(th)
    out = f64(base).copy()
    out[:, idx] = new.reshape(C, N)
    return out

@@ -1,0 +1,55 @@
+import math
+
+import concourse.mybir as mybir
+
+F32 = mybir.dt.float32
+U16 = mybir.dt.uint16
+MULT = mybir.AluOpType.mult
+ADD = mybir.AluOpType.add
+SIN = mybir.ActivationFunctionType.Sin
+
+HEADS = 2
+D = 128
+HALF = D // 2
+SLOTS = 512
+N = 256
+
+
+def tile_gqa_kernel(tc, base, k, theta, offs, out):
+    nc = tc.nc
+    with (
+        tc.tile_pool(name="held", bufs=1) as held,
+        tc.tile_pool(name="per_head", bufs=HEADS) as per_head,
+    ):
+        offsets = held.tile([D, N // 16], U16, name="offsets")
+        nc.sync.dma_start(offsets[:], offs)
+
+        angle = held.tile([D, N], F32, name="angle")
+        nc.sync.dma_start(angle[:], theta)
+
+        sign = held.tile([D, 1], F32, name="sign")
+        nc.gpsimd.memset(sign[0:HALF, :], -1.0)
+        nc.gpsimd.memset(sign[HALF:D, :], 1.0)
+
+        signed_sine = held.tile([D, N], F32, name="signed_sine")
+        nc.scalar.activation(signed_sine[:], angle[:], SIN, scale=sign[:])
+        cosine = held.tile([D, N], F32, name="cosine")
+        nc.scalar.activation(cosine[:], angle[:], SIN, bias=math.pi / 2)
+
+        for h in range(HEADS):
+            first = h * D
+            window = per_head.tile([D, SLOTS], F32, name="window")
+            nc.sync.dma_start(window[:], base[first : first + D, :])
+            key = per_head.tile([D, N], F32, name="key")
+            nc.sync.dma_start(key[:], k[first : first + D, :])
+            swapped = per_head.tile([D, N], F32, name="swapped")
+            nc.scalar.dma_start(swapped[0:HALF, :], k[first + HALF : first + D, :])
+            nc.scalar.dma_start(swapped[HALF:D, :], k[first : first + HALF, :])
+
+            with_cosine = per_head.tile([D, N], F32, name="with_cosine")
+            nc.vector.tensor_tensor(with_cosine[:], key[:], cosine[:], MULT)
+            with_sine = per_head.tile([D, N], F32, name="with_sine")
+            nc.vector.tensor_tensor(with_sine[:], swapped[:], signed_sine[:], MULT)
+
+            nc.vector.tensor_tensor(window[:].indirect(offsets[:]), with_cosine[:], with_sine[:], ADD)
+            nc.sync.dma_start(out[first : first + D, :], window[:])

@@ -21,15 +21,18 @@ def tile_gqa_kernel(tc, base, k, theta, offs, out):
         tc.tile_pool(name="held", bufs=1) as held,
         tc.tile_pool(name="per_head", bufs=HEADS) as per_head,
     ):
-        offsets = held.tile([D, N // 16], U16, name="offsets")
-        nc.sync.dma_start(offsets[:], offs)
-
         angle = held.tile([D, N], F32, name="angle")
         nc.sync.dma_start(angle[:], theta)
 
+        offsets = held.tile([D, N // 16], U16, name="offsets")
+        nc.sync.dma_start(offsets[:], offs)
+
         sign = held.tile([D, 1], F32, name="sign")
-        nc.gpsimd.memset(sign[0:HALF, :], -1.0)
-        nc.gpsimd.memset(sign[HALF:D, :], 1.0)
+        nc.vector.memset(sign[0:HALF, :], -1.0)
+        nc.vector.memset(sign[HALF:D, :], 1.0)
+
+        warm = held.tile([D, 1], F32, name="warm")
+        nc.scalar.activation(warm[:], sign[:], SIN)
 
         signed_sine = held.tile([D, N], F32, name="signed_sine")
         nc.scalar.activation(signed_sine[:], angle[:], SIN, scale=sign[:])

@@ -49,10 +49,11 @@ def tile_gqa_kernel(tc, base, k, theta, offs, out):
             nc.scalar.dma_start(swapped[0:HALF, :], k[first + HALF : first + D, :])
             nc.scalar.dma_start(swapped[HALF:D, :], k[first : first + HALF, :])
 
-            with_cosine = per_head.tile([D, N], F32, name="with_cosine")
-            nc.vector.tensor_tensor(with_cosine[:], key[:], cosine[:], MULT)
+            multiplier = nc.vector if h == 0 else nc.gpsimd
             with_sine = per_head.tile([D, N], F32, name="with_sine")
-            nc.vector.tensor_tensor(with_sine[:], swapped[:], signed_sine[:], MULT)
+            multiplier.tensor_tensor(with_sine[:], swapped[:], signed_sine[:], MULT)
+            with_cosine = per_head.tile([D, N], F32, name="with_cosine")
+            multiplier.tensor_tensor(with_cosine[:], key[:], cosine[:], MULT)
 
             nc.vector.tensor_tensor(window[:].indirect(offsets[:]), with_cosine[:], with_sine[:], ADD)
             nc.sync.dma_start(out[first : first + D, :], window[:])

@@ -17,15 +17,21 @@ N = 256
 
 def tile_gqa_kernel(tc, base, k, theta, offs, out):
     nc = tc.nc
-    with (
-        tc.tile_pool(name="held", bufs=1) as held,
-        tc.tile_pool(name="per_head", bufs=HEADS) as per_head,
-    ):
+    k_by_head = k.rearrange("(h d) n -> d h n", d=D)
+    with tc.tile_pool(name="held", bufs=1) as held:
         angle = held.tile([D, N], F32, name="angle")
-        nc.sync.dma_start(angle[:], theta)
-
         offsets = held.tile([D, N // 16], U16, name="offsets")
+        key = held.tile([D, HEADS, N], F32, name="key")
+        swapped = held.tile([D, HEADS, N], F32, name="swapped")
+        window = [held.tile([D, SLOTS], F32, name=f"window{h}") for h in range(HEADS)]
+
+        nc.sync.dma_start(angle[:], theta)
+        nc.scalar.dma_start(swapped[0:HALF, :, :], k_by_head[HALF:D, :, :])
+        nc.sync.dma_start(swapped[HALF:D, :, :], k_by_head[0:HALF, :, :])
+        nc.sync.dma_start(key[:], k_by_head)
+        nc.sync.dma_start(window[0][:], base[0:D, :])
         nc.sync.dma_start(offsets[:], offs)
+        nc.sync.dma_start(window[1][:], base[D : 2 * D, :])
 
         sign = held.tile([D, 1], F32, name="sign")
         nc.vector.memset(sign[0:HALF, :], -1.0)
@@ -39,21 +45,12 @@ def tile_gqa_kernel(tc, base, k, theta, offs, out):
         cosine = held.tile([D, N], F32, name="cosine")
         nc.scalar.activation(cosine[:], angle[:], SIN, bias=math.pi / 2)
 
+        both_heads = [D, HEADS, N]
+        with_sine = held.tile(both_heads, F32, name="with_sine")
+        nc.vector.tensor_tensor(with_sine[:], swapped[:], signed_sine[:].unsqueeze(1).to_broadcast(both_heads), MULT)
+        with_cosine = held.tile(both_heads, F32, name="with_cosine")
+        nc.vector.tensor_tensor(with_cosine[:], key[:], cosine[:].unsqueeze(1).to_broadcast(both_heads), MULT)
+
         for h in range(HEADS):
-            first = h * D
-            window = per_head.tile([D, SLOTS], F32, name="window")
-            nc.sync.dma_start(window[:], base[first : first + D, :])
-            key = per_head.tile([D, N], F32, name="key")
-            nc.sync.dma_start(key[:], k[first : first + D, :])
-            swapped = per_head.tile([D, N], F32, name="swapped")
-            nc.scalar.dma_start(swapped[0:HALF, :], k[first + HALF : first + D, :])
-            nc.scalar.dma_start(swapped[HALF:D, :], k[first : first + HALF, :])
-
-            multiplier = nc.vector if h == 0 else nc.gpsimd
-            with_sine = per_head.tile([D, N], F32, name="with_sine")
-            multiplier.tensor_tensor(with_sine[:], swapped[:], signed_sine[:], MULT)
-            with_cosine = per_head.tile([D, N], F32, name="with_cosine")
-            multiplier.tensor_tensor(with_cosine[:], key[:], cosine[:], MULT)
-
-            nc.vector.tensor_tensor(window[:].indirect(offsets[:]), with_cosine[:], with_sine[:], ADD)
-            nc.sync.dma_start(out[first : first + D, :], window[:])
+            nc.vector.tensor_tensor(window[h][:].indirect(offsets[:]), with_cosine[:, h, :], with_sine[:, h, :], ADD)
+            nc.sync.dma_start(out[h * D : (h + 1) * D, :], window[h][:])

@@ -49,7 +49,8 @@ def tile_gqa_kernel(tc, base, k, theta, offs, out):
         with_sine = held.tile(both_heads, F32, name="with_sine")
         nc.vector.tensor_tensor(with_sine[:], swapped[:], signed_sine[:].unsqueeze(1).to_broadcast(both_heads), MULT)
         with_cosine = held.tile(both_heads, F32, name="with_cosine")
-        nc.vector.tensor_tensor(with_cosine[:], key[:], cosine[:].unsqueeze(1).to_broadcast(both_heads), MULT)
+        for h in range(HEADS):
+            nc.vector.tensor_tensor(with_cosine[:, h, :], key[:, h, :], cosine[:], MULT)
 
         for h in range(HEADS):
             nc.vector.tensor_tensor(window[h][:].indirect(offsets[:]), with_cosine[:, h, :], with_sine[:, h, :], ADD)

@@ -41,13 +41,21 @@ def tile_gqa_kernel(tc, base, k, theta, offs, out):
         nc.scalar.activation(warm[:], sign[:], SIN)
 
         signed_sine = held.tile([D, N], F32, name="signed_sine")
-        nc.scalar.activation(signed_sine[:], angle[:], SIN, scale=sign[:])
+        pieces = [slice(0, N // 2), slice(N // 2, N)]
+        for piece in pieces:
+            nc.scalar.activation(signed_sine[:, piece], angle[:, piece], SIN, scale=sign[:])
         cosine = held.tile([D, N], F32, name="cosine")
         nc.scalar.activation(cosine[:], angle[:], SIN, bias=math.pi / 2)
 
         both_heads = [D, HEADS, N]
         with_sine = held.tile(both_heads, F32, name="with_sine")
-        nc.vector.tensor_tensor(with_sine[:], swapped[:], signed_sine[:].unsqueeze(1).to_broadcast(both_heads), MULT)
+        for piece in pieces:
+            nc.vector.tensor_tensor(
+                with_sine[:, :, piece],
+                swapped[:, :, piece],
+                signed_sine[:, piece].unsqueeze(1).to_broadcast([D, HEADS, N // 2]),
+                MULT,
+            )
         with_cosine = held.tile(both_heads, F32, name="with_cosine")
         for h in range(HEADS):
             nc.vector.tensor_tensor(with_cosine[:, h, :], key[:, h, :], cosine[:], MULT)

@@ -9,57 +9,62 @@ ADD = mybir.AluOpType.add
 SIN = mybir.ActivationFunctionType.Sin
 
 HEADS = 2
-D = 128
-HALF = D // 2
+SIDES = 2
+HALF = 64
+P = HEADS * HALF
 SLOTS = 512
 N = 256
 
 
 def tile_gqa_kernel(tc, base, k, theta, offs, out):
     nc = tc.nc
-    k_by_head = k.rearrange("(h d) n -> d h n", d=D)
+
+    def rows(dram, h, side):
+        first = (h * SIDES + side) * HALF
+        return dram[first : first + HALF, :]
+
     with tc.tile_pool(name="held", bufs=1) as held:
-        angle = held.tile([D, N], F32, name="angle")
-        offsets = held.tile([D, N // 16], U16, name="offsets")
-        key = held.tile([D, HEADS, N], F32, name="key")
-        swapped = held.tile([D, HEADS, N], F32, name="swapped")
-        window = [held.tile([D, SLOTS], F32, name=f"window{h}") for h in range(HEADS)]
+        angle = held.tile([P, N], F32, name="angle")
+        offsets = held.tile([P, N // 16], U16, name="offsets")
+        key = held.tile([P, SIDES, N], F32, name="key")
+        window = [held.tile([P, SLOTS], F32, name=f"window{side}") for side in range(SIDES)]
 
-        nc.sync.dma_start(angle[:], theta)
-        nc.scalar.dma_start(swapped[0:HALF, :, :], k_by_head[HALF:D, :, :])
-        nc.sync.dma_start(swapped[HALF:D, :, :], k_by_head[0:HALF, :, :])
-        nc.sync.dma_start(key[:], k_by_head)
-        nc.sync.dma_start(window[0][:], base[0:D, :])
-        nc.sync.dma_start(offsets[:], offs)
-        nc.sync.dma_start(window[1][:], base[D : 2 * D, :])
-
-        sign = held.tile([D, 1], F32, name="sign")
-        nc.vector.memset(sign[0:HALF, :], -1.0)
-        nc.vector.memset(sign[HALF:D, :], 1.0)
-
-        warm = held.tile([D, 1], F32, name="warm")
-        nc.scalar.activation(warm[:], sign[:], SIN)
-
-        signed_sine = held.tile([D, N], F32, name="signed_sine")
-        pieces = [slice(0, N // 2), slice(N // 2, N)]
-        for piece in pieces:
-            nc.scalar.activation(signed_sine[:, piece], angle[:, piece], SIN, scale=sign[:])
-        cosine = held.tile([D, N], F32, name="cosine")
-        nc.scalar.activation(cosine[:], angle[:], SIN, bias=math.pi / 2)
-
-        both_heads = [D, HEADS, N]
-        with_sine = held.tile(both_heads, F32, name="with_sine")
-        for piece in pieces:
-            nc.vector.tensor_tensor(
-                with_sine[:, :, piece],
-                swapped[:, :, piece],
-                signed_sine[:, piece].unsqueeze(1).to_broadcast([D, HEADS, N // 2]),
-                MULT,
+        for h in range(HEADS):
+            nc.sync.dma_start(angle[h:P:HEADS, :], theta[h * HALF : (h + 1) * HALF, :])
+        for h in range(HEADS):
+            nc.sync.dma_start(
+                key[h:P:HEADS, :, :],
+                k[h * SIDES * HALF : (h + 1) * SIDES * HALF, :].rearrange("(s d) n -> d s n", s=SIDES),
             )
-        with_cosine = held.tile(both_heads, F32, name="with_cosine")
         for h in range(HEADS):
-            nc.vector.tensor_tensor(with_cosine[:, h, :], key[:, h, :], cosine[:], MULT)
+            nc.sync.dma_start(window[0][h:P:HEADS, :], rows(base, h, 0))
+        nc.sync.dma_start(offsets[:], offs)
+        for h in range(HEADS):
+            nc.sync.dma_start(window[1][h:P:HEADS, :], rows(base, h, 1))
 
-        for h in range(HEADS):
-            nc.vector.tensor_tensor(window[h][:].indirect(offsets[:]), with_cosine[:, h, :], with_sine[:, h, :], ADD)
-            nc.sync.dma_start(out[h * D : (h + 1) * D, :], window[h][:])
+        ready = held.tile([P, 1], F32, name="ready")
+        nc.gpsimd.memset(ready[:], 0.0)
+        warm = held.tile([P, 1], F32, name="warm")
+        nc.scalar.activation(warm[:], ready[:], SIN)
+
+        minus_sine = held.tile([P, N], F32, name="minus_sine")
+        cosine = held.tile([P, N], F32, name="cosine")
+        sine = held.tile([P, N], F32, name="sine")
+        nc.scalar.activation(minus_sine[:], angle[:], SIN, scale=-1.0)
+        nc.scalar.activation(cosine[:], angle[:], SIN, bias=math.pi / 2)
+        nc.scalar.activation(sine[:], angle[:], SIN)
+
+        with_sine = held.tile([P, SIDES, N], F32, name="with_sine")
+        with_cosine = held.tile([P, SIDES, N], F32, name="with_cosine")
+        nc.vector.tensor_tensor(with_sine[:, 0, :], key[:, 1, :], minus_sine[:], MULT)
+        nc.vector.tensor_tensor(
+            with_cosine[:], key[:], cosine[:].unsqueeze(1).to_broadcast([P, SIDES, N]), MULT
+        )
+        nc.vector.tensor_tensor(with_sine[:, 1, :], key[:, 0, :], sine[:], MULT)
+
+        for side in range(SIDES):
+            nc.vector.tensor_tensor(
+                window[side][:].indirect(offsets[:]), with_cosine[:, side, :], with_sine[:, side, :], ADD
+            )
+            for h in range(HEADS):
+                nc.sync.dma_start(rows(out, h, side), window[side][h:P:HEADS, :])

@@ -47,19 +47,25 @@ def tile_gqa_kernel(tc, base, k, theta, offs, out):
         warm = held.tile([P, 1], F32, name="warm")
         nc.scalar.activation(warm[:], ready[:], SIN)
 
-        minus_sine = held.tile([P, N], F32, name="minus_sine")
         cosine = held.tile([P, N], F32, name="cosine")
+        minus_sine = held.tile([P, N], F32, name="minus_sine")
         sine = held.tile([P, N], F32, name="sine")
+        pieces = [slice(0, N // 2), slice(N // 2, N)]
+        for piece in pieces:
+            nc.scalar.activation(cosine[:, piece], angle[:, piece], SIN, bias=math.pi / 2)
         nc.scalar.activation(minus_sine[:], angle[:], SIN, scale=-1.0)
-        nc.scalar.activation(cosine[:], angle[:], SIN, bias=math.pi / 2)
         nc.scalar.activation(sine[:], angle[:], SIN)
 
         with_sine = held.tile([P, SIDES, N], F32, name="with_sine")
         with_cosine = held.tile([P, SIDES, N], F32, name="with_cosine")
+        for piece in pieces:
+            nc.vector.tensor_tensor(
+                with_cosine[:, :, piece],
+                key[:, :, piece],
+                cosine[:, piece].unsqueeze(1).to_broadcast([P, SIDES, N // 2]),
+                MULT,
+            )
         nc.vector.tensor_tensor(with_sine[:, 0, :], key[:, 1, :], minus_sine[:], MULT)
-        nc.vector.tensor_tensor(
-            with_cosine[:], key[:], cosine[:].unsqueeze(1).to_broadcast([P, SIDES, N]), MULT
-        )
         nc.vector.tensor_tensor(with_sine[:, 1, :], key[:, 0, :], sine[:], MULT)
 
         for side in range(SIDES):

@@ -31,11 +31,13 @@ def tile_gqa_kernel(tc, base, k, theta, offs, out):
 
         for h in range(HEADS):
             nc.sync.dma_start(angle[h:P:HEADS, :], theta[h * HALF : (h + 1) * HALF, :])
-        for h in range(HEADS):
-            nc.sync.dma_start(
-                key[h:P:HEADS, :, :],
-                k[h * SIDES * HALF : (h + 1) * SIDES * HALF, :].rearrange("(s d) n -> d s n", s=SIDES),
-            )
+        pieces = [slice(0, N // 2), slice(N // 2, N)]
+        for piece in pieces:
+            for h in range(HEADS):
+                nc.sync.dma_start(
+                    key[h:P:HEADS, :, piece],
+                    k[h * SIDES * HALF : (h + 1) * SIDES * HALF, piece].rearrange("(s d) n -> d s n", s=SIDES),
+                )
         for h in range(HEADS):
             nc.sync.dma_start(window[0][h:P:HEADS, :], rows(base, h, 0))
         nc.sync.dma_start(offsets[:], offs)
@@ -50,7 +52,6 @@ def tile_gqa_kernel(tc, base, k, theta, offs, out):
         cosine = held.tile([P, N], F32, name="cosine")
         minus_sine = held.tile([P, N], F32, name="minus_sine")
         sine = held.tile([P, N], F32, name="sine")
-        pieces = [slice(0, N // 2), slice(N // 2, N)]
         for piece in pieces:
             nc.scalar.activation(cosine[:, piece], angle[:, piece], SIN, bias=math.pi / 2)
         nc.scalar.activation(minus_sine[:], angle[:], SIN, scale=-1.0)

@@ -19,9 +19,10 @@ N = 256
 def tile_gqa_kernel(tc, base, k, theta, offs, out):
     nc = tc.nc
 
-    def rows(dram, h, side):
-        first = (h * SIDES + side) * HALF
-        return dram[first : first + HALF, :]
+    theta_by_pair = theta.rearrange("(h d) n -> d h n", h=HEADS)
+    k_by_pair = k.rearrange("(hs d) n -> d hs n", d=HALF)
+    base_by_pair = base.rearrange("(h s d) n -> d h s n", h=HEADS, s=SIDES)
+    out_by_pair = out.rearrange("(h s d) n -> d h s n", h=HEADS, s=SIDES)
 
     with tc.tile_pool(name="held", bufs=1) as held:
         angle = held.tile([P, N], F32, name="angle")
@@ -29,20 +30,13 @@ def tile_gqa_kernel(tc, base, k, theta, offs, out):
         key = held.tile([P, SIDES, N], F32, name="key")
         window = [held.tile([P, SLOTS], F32, name=f"window{side}") for side in range(SIDES)]
 
-        for h in range(HEADS):
-            nc.sync.dma_start(angle[h:P:HEADS, :], theta[h * HALF : (h + 1) * HALF, :])
         pieces = [slice(0, N // 2), slice(N // 2, N)]
+        nc.sync.dma_start(angle[:], theta_by_pair)
         for piece in pieces:
-            for h in range(HEADS):
-                nc.sync.dma_start(
-                    key[h:P:HEADS, :, piece],
-                    k[h * SIDES * HALF : (h + 1) * SIDES * HALF, piece].rearrange("(s d) n -> d s n", s=SIDES),
-                )
-        for h in range(HEADS):
-            nc.sync.dma_start(window[0][h:P:HEADS, :], rows(base, h, 0))
+            nc.sync.dma_start(key[:, :, piece], k_by_pair[:, :, piece])
+        nc.sync.dma_start(window[0][:], base_by_pair[:, :, 0, :])
         nc.sync.dma_start(offsets[:], offs)
-        for h in range(HEADS):
-            nc.sync.dma_start(window[1][h:P:HEADS, :], rows(base, h, 1))
+        nc.sync.dma_start(window[1][:], base_by_pair[:, :, 1, :])
 
         ready = held.tile([P, 1], F32, name="ready")
         nc.gpsimd.memset(ready[:], 0.0)
@@ -73,5 +67,4 @@ def tile_gqa_kernel(tc, base, k, theta, offs, out):
             nc.vector.tensor_tensor(
                 window[side][:].indirect(offsets[:]), with_cosine[:, side, :], with_sine[:, side, :], ADD
             )
-            for h in range(HEADS):
-                nc.sync.dma_start(rows(out, h, side), window[side][h:P:HEADS, :])
+            nc.sync.dma_start(out_by_pair[:, :, side, :], window[side][:])

@@ -34,8 +34,8 @@ def tile_gqa_kernel(tc, base, k, theta, offs, out):
         nc.sync.dma_start(angle[:], theta_by_pair)
         for piece in pieces:
             nc.sync.dma_start(key[:, :, piece], k_by_pair[:, :, piece])
-        nc.sync.dma_start(window[0][:], base_by_pair[:, :, 0, :])
         nc.sync.dma_start(offsets[:], offs)
+        nc.sync.dma_start(window[0][:], base_by_pair[:, :, 0, :])
         nc.sync.dma_start(window[1][:], base_by_pair[:, :, 1, :])
 
         ready = held.tile([P, 1], F32, name="ready")

@@ -48,7 +48,7 @@ def tile_gqa_kernel(tc, base, k, theta, offs, out):
         sine = held.tile([P, N], F32, name="sine")
         for piece in pieces:
             nc.scalar.activation(cosine[:, piece], angle[:, piece], SIN, bias=math.pi / 2)
-        nc.scalar.activation(minus_sine[:], angle[:], SIN, scale=-1.0)
+            nc.scalar.activation(minus_sine[:, piece], angle[:, piece], SIN, scale=-1.0)
         nc.scalar.activation(sine[:], angle[:], SIN)
 
         with_sine = held.tile([P, SIDES, N], F32, name="with_sine")
@@ -60,7 +60,7 @@ def tile_gqa_kernel(tc, base, k, theta, offs, out):
                 cosine[:, piece].unsqueeze(1).to_broadcast([P, SIDES, N // 2]),
                 MULT,
             )
-        nc.vector.tensor_tensor(with_sine[:, 0, :], key[:, 1, :], minus_sine[:], MULT)
+            nc.vector.tensor_tensor(with_sine[:, 0, piece], key[:, 1, piece], minus_sine[:, piece], MULT)
         nc.vector.tensor_tensor(with_sine[:, 1, :], key[:, 0, :], sine[:], MULT)
 
         for side in range(SIDES):

@@ -20,7 +20,7 @@ def tile_gqa_kernel(tc, base, k, theta, offs, out):
     nc = tc.nc
 
     theta_by_pair = theta.rearrange("(h d) n -> d h n", h=HEADS)
-    k_by_pair = k.rearrange("(hs d) n -> d hs n", d=HALF)
+    k_by_pair = k.rearrange("(h s d) n -> d h s n", h=HEADS, s=SIDES)
     base_by_pair = base.rearrange("(h s d) n -> d h s n", h=HEADS, s=SIDES)
     out_by_pair = out.rearrange("(h s d) n -> d h s n", h=HEADS, s=SIDES)
 
@@ -30,10 +30,9 @@ def tile_gqa_kernel(tc, base, k, theta, offs, out):
         key = held.tile([P, SIDES, N], F32, name="key")
         window = [held.tile([P, SLOTS], F32, name=f"window{side}") for side in range(SIDES)]
 
-        pieces = [slice(0, N // 2), slice(N // 2, N)]
         nc.sync.dma_start(angle[:], theta_by_pair)
-        for piece in pieces:
-            nc.sync.dma_start(key[:, :, piece], k_by_pair[:, :, piece])
+        for side in (1, 0):
+            nc.sync.dma_start(key[:, side, :], k_by_pair[:, :, side, :])
         nc.sync.dma_start(offsets[:], offs)
         nc.sync.dma_start(window[0][:], base_by_pair[:, :, 0, :])
         nc.sync.dma_start(window[1][:], base_by_pair[:, :, 1, :])
@@ -46,6 +45,7 @@ def tile_gqa_kernel(tc, base, k, theta, offs, out):
         cosine = held.tile([P, N], F32, name="cosine")
         minus_sine = held.tile([P, N], F32, name="minus_sine")
         sine = held.tile([P, N], F32, name="sine")
+        pieces = [slice(0, N // 2), slice(N // 2, N)]
         for piece in pieces:
             nc.scalar.activation(cosine[:, piece], angle[:, piece], SIN, bias=math.pi / 2)
             nc.scalar.activation(minus_sine[:, piece], angle[:, piece], SIN, scale=-1.0)
@@ -54,13 +54,9 @@ def tile_gqa_kernel(tc, base, k, theta, offs, out):
         with_sine = held.tile([P, SIDES, N], F32, name="with_sine")
         with_cosine = held.tile([P, SIDES, N], F32, name="with_cosine")
         for piece in pieces:
-            nc.vector.tensor_tensor(
-                with_cosine[:, :, piece],
-                key[:, :, piece],
-                cosine[:, piece].unsqueeze(1).to_broadcast([P, SIDES, N // 2]),
-                MULT,
-            )
+            nc.vector.tensor_tensor(with_cosine[:, 1, piece], key[:, 1, piece], cosine[:, piece], MULT)
             nc.vector.tensor_tensor(with_sine[:, 0, piece], key[:, 1, piece], minus_sine[:, piece], MULT)
+        nc.vector.tensor_tensor(with_cosine[:, 0, :], key[:, 0, :], cosine[:], MULT)
         nc.vector.tensor_tensor(with_sine[:, 1, :], key[:, 0, :], sine[:], MULT)
 
         for side in range(SIDES):

import math

import concourse.mybir as mybir

F32 = mybir.dt.float32
U16 = mybir.dt.uint16
MULT = mybir.AluOpType.mult
ADD = mybir.AluOpType.add
SIN = mybir.ActivationFunctionType.Sin

HEADS = 2
SIDES = 2
HALF = 64
P = HEADS * HALF
SLOTS = 512
N = 256


def tile_gqa_kernel(tc, base, k, theta, offs, out):
    nc = tc.nc

    theta_by_pair = theta.rearrange("(h d) n -> d h n", h=HEADS)
    k_by_pair = k.rearrange("(h s d) n -> d h s n", h=HEADS, s=SIDES)
    base_by_pair = base.rearrange("(h s d) n -> d h s n", h=HEADS, s=SIDES)
    out_by_pair = out.rearrange("(h s d) n -> d h s n", h=HEADS, s=SIDES)

    with tc.tile_pool(name="held", bufs=1) as held:
        angle = held.tile([P, N], F32, name="angle")
        offsets = held.tile([P, N // 16], U16, name="offsets")
        key = held.tile([P, SIDES, N], F32, name="key")
        window = [held.tile([P, SLOTS], F32, name=f"window{side}") for side in range(SIDES)]

        nc.sync.dma_start(angle[:], theta_by_pair)
        for side in (1, 0):
            nc.sync.dma_start(key[:, side, :], k_by_pair[:, :, side, :])
        nc.sync.dma_start(offsets[:], offs)
        nc.sync.dma_start(window[0][:], base_by_pair[:, :, 0, :])
        nc.sync.dma_start(window[1][:], base_by_pair[:, :, 1, :])

        ready = held.tile([P, 1], F32, name="ready")
        nc.gpsimd.memset(ready[:], 0.0)
        warm = held.tile([P, 1], F32, name="warm")
        nc.scalar.activation(warm[:], ready[:], SIN)

        cosine = held.tile([P, N], F32, name="cosine")
        minus_sine = held.tile([P, N], F32, name="minus_sine")
        sine = held.tile([P, N], F32, name="sine")
        pieces = [slice(0, N // 2), slice(N // 2, N)]
        for piece in pieces:
            nc.scalar.activation(cosine[:, piece], angle[:, piece], SIN, bias=math.pi / 2)
            nc.scalar.activation(minus_sine[:, piece], angle[:, piece], SIN, scale=-1.0)
        nc.scalar.activation(sine[:], angle[:], SIN)

        with_sine = held.tile([P, SIDES, N], F32, name="with_sine")
        with_cosine = held.tile([P, SIDES, N], F32, name="with_cosine")
        for piece in pieces:
            nc.vector.tensor_tensor(with_cosine[:, 1, piece], key[:, 1, piece], cosine[:, piece], MULT)
            nc.vector.tensor_tensor(with_sine[:, 0, piece], key[:, 1, piece], minus_sine[:, piece], MULT)
        nc.vector.tensor_tensor(with_cosine[:, 0, :], key[:, 0, :], cosine[:], MULT)
        nc.vector.tensor_tensor(with_sine[:, 1, :], key[:, 0, :], sine[:], MULT)

        for side in range(SIDES):
            nc.vector.tensor_tensor(
                window[side][:].indirect(offsets[:]), with_cosine[:, side, :], with_sine[:, side, :], ADD
            )
            nc.sync.dma_start(out_by_pair[:, :, side, :], window[side][:])
